import numpy as np
import ml_dtypes


def mxq(x, axis, fmt="e4m3"):
    dtype, down = {"e4m3": (ml_dtypes.float8_e4m3fn, 7), "e5m2": (ml_dtypes.float8_e5m2, 14)}[fmt]
    v = np.moveaxis(np.asarray(x, np.float32).astype(ml_dtypes.bfloat16).astype(np.float64), axis, -1)
    blocks = v.reshape(v.shape[:-1] + (-1, 32))
    amax = np.abs(blocks).max(-1, keepdims=True)
    byte = np.maximum(np.where(amax > 0, np.frexp(amax)[1] - 1 + 127, 0) - down, 1)
    scale = np.exp2(byte - 127.0)
    codes = (blocks / scale).astype(np.float32).astype(dtype).astype(np.float64)
    return np.moveaxis((codes * scale).reshape(v.shape), -1, axis)


WIDE = False


def mx_kscale(k):
    if not WIDE:
        return np.ones(k)
    levels = np.array([10, -10, 5, -5, 0])
    if k % 512:
        return np.exp2(np.random.permutation(np.resize(levels, k // 32))).repeat(32)
    a = np.empty((k // 512, 16))
    for p in range(k // 512):
        a[p, :8] = np.random.permutation(np.resize(levels, 8))
        for g in range(8):
            far = levels[np.abs(levels - a[p, g]) >= 10]
            a[p, g + 8] = far[np.random.randint(len(far))]
    return np.exp2(a.ravel()).repeat(32)


BF16 = ml_dtypes.bfloat16


def bf(x):
    return np.asarray(x, np.float32).astype(BF16)


def f64(x):
    return np.asarray(x).astype(np.float64)


B, T, C, KW = 4, 1024, 1024, 3
PAD = KW // 2


def setup_inputs():
    s = mx_kscale(C)
    return {"x": bf(np.random.standard_normal((B, T, C)) * s),
            "w1": bf(np.random.standard_normal((C, C)) / np.sqrt(C) / s[None, :]),
            "b1": bf(np.random.standard_normal(C) * 0.2),
            "w2": bf(np.random.standard_normal((C, KW)) * 0.8),
            "b2": bf(np.random.standard_normal(C) * 0.2)}


def reference(x, w1, b1, w2, b2):
    h = (mxq(f64(x), 2, "e4m3") @ mxq(f64(w1), 1, "e4m3").T) + f64(b1)
    hp = np.pad(h, ((0, 0), (PAD, PAD), (0, 0)))
    taps = f64(w2)
    y = hp[:, 0:T, :] * taps[:, 0]
    for j in range(1, KW):
        y = y + hp[:, j:j + T, :] * taps[:, j]
    return y + f64(b2)

@@ -1,0 +1,256 @@
+from contextlib import ExitStack
+
+import concourse.mybir as mybir
+from concourse.masks import make_identity
+
+F32 = mybir.dt.float32
+BF16 = mybir.dt.bfloat16
+U32 = mybir.dt.uint32
+U8 = mybir.dt.uint8
+FP8X4 = mybir.dt.float8_e4m3fn_x4
+ALU = mybir.AluOpType
+ACT = mybir.ActivationFunctionType
+
+B, T, C, D, KW = 4, 1024, 1024, 1024, 3
+P = 128
+PACK = 4
+K_PASS = P * PACK
+PASSES = C // K_PASS
+PAIRS = PACK // 2
+BANK = 512
+T_BANKS = T // BANK
+T_BLOCKS = T // P
+X_BLOCKS = B * T_BLOCKS
+BANK_BLOCKS = BANK // P
+D_TILES = D // P
+LOAD_BLOCKS = 2
+STORE_TILES = 2
+
+STEPS = B * D_TILES
+X_AHEAD = T_BLOCKS + 1
+W_AHEAD = 2
+BACK_LAG = 3
+VECTOR_EVERY = 3
+
+FLOPS = 2 * B * T * C * D + 2 * KW * B * T * D
+
+
+def tile_cvim_pa_t_kernel(tc, x, w1, b1, w2, b2, out):
+    nc = tc.nc
+    with ExitStack() as pools:
+        pools.enter_context(tc.manual_schedule())
+        consts = pools.enter_context(tc.tile_pool(name="consts", bufs=1))
+        raws = pools.enter_context(tc.tile_pool(name="raws", bufs=1))
+        groups = pools.enter_context(tc.tile_pool(name="groups", bufs=2))
+        codes = pools.enter_context(tc.tile_pool(name="codes", bufs=2 * T_BANKS))
+        ys = pools.enter_context(tc.tile_pool(name="ys", bufs=BACK_LAG + 2))
+        outs = pools.enter_context(tc.tile_pool(name="outs", bufs=3))
+        accs = pools.enter_context(tc.psum_pool(name="accs", bufs=5))
+        turns = pools.enter_context(tc.psum_pool(name="turns", bufs=3))
+
+        rows_bf16 = consts.tile([P, (2 + KW) * P], BF16)
+        nc.gpsimd.memset(rows_bf16[:], 0.0)
+        nc.sync.dma_start(out=rows_bf16[0:D_TILES, 0:P], in_=b1.rearrange("(e p) -> e p", p=P))
+        nc.sync.dma_start(out=rows_bf16[0:D_TILES, P : 2 * P], in_=b2.rearrange("(e p) -> e p", p=P))
+        nc.sync.dma_start(
+            out=rows_bf16[0:D_TILES, 2 * P : (2 + KW) * P], in_=w2.rearrange("(e p) j -> e (p j)", p=P)
+        )
+
+        x_rows = x.flatten_outer_dims()
+        x_raw = raws.tile([P, X_BLOCKS * C], BF16)
+        w_raw = raws.tile([P, D_TILES * C], BF16)
+
+        def load_rows(raw, rows, first):
+            nc.sync.dma_start(
+                out=raw[:].rearrange("p (k c) -> p k c", c=C)[:, first : first + LOAD_BLOCKS, :],
+                in_=rows[first * P : (first + LOAD_BLOCKS) * P, :].rearrange("(k p) c -> p k c", p=P),
+            )
+
+        for first in range(0, T_BLOCKS, LOAD_BLOCKS):
+            load_rows(x_raw, x_rows, first)
+        for first in range(0, D_TILES, LOAD_BLOCKS):
+            load_rows(w_raw, w1, first)
+            load_rows(x_raw, x_rows, T_BLOCKS + first)
+        for first in range(2 * T_BLOCKS, X_BLOCKS, LOAD_BLOCKS):
+            load_rows(x_raw, x_rows, first)
+
+        ident = consts.tile([P, P], F32)
+        make_identity(nc, ident[:])
+
+        rows_f32 = consts.tile([P, 2 + KW, P], F32)
+        nc.vector.tensor_copy(
+            out=rows_f32[:, 0:2, :], in_=rows_bf16[:, 0 : 2 * P].rearrange("e (v p) -> e v p", v=2)
+        )
+        nc.vector.tensor_copy(
+            out=rows_f32[:, 2 : 2 + KW, :],
+            in_=rows_bf16[:, 2 * P : (2 + KW) * P].rearrange("e (p j) -> e j p", j=KW),
+        )
+        chan = consts.tile([P, 2 + KW, D_TILES], F32)
+        for v in range(2 + KW):
+            column = turns.tile([P, P], F32, tag="turn")
+            nc.tensor.transpose(column[:], rows_f32[:, v, :], ident[:])
+            nc.vector.tensor_copy(out=chan[:, v, :], in_=column[:, 0:D_TILES])
+        bias1 = chan[:, 0, :]
+        bias2 = chan[:, 1, :]
+        tap_sum = consts.tile([P, D_TILES], F32)
+        nc.vector.tensor_tensor(out=tap_sum[:], in0=chan[:, 2, :], in1=chan[:, 3, :], op=ALU.add)
+        nc.vector.tensor_tensor(out=tap_sum[:], in0=tap_sum[:], in1=chan[:, 4, :], op=ALU.add)
+        bias_all = consts.tile([P, D_TILES], F32)
+        nc.vector.tensor_tensor(out=bias_all[:], in0=tap_sum[:], in1=bias1, op=ALU.mult)
+        nc.vector.tensor_tensor(out=bias_all[:], in0=bias_all[:], in1=bias2, op=ALU.add)
+        edge_fix = consts.tile([P, D_TILES, 2], F32)
+        for side in range(2):
+            nc.vector.scalar_tensor_tensor(
+                out=edge_fix[:, :, side],
+                in0=bias1,
+                scalar=-1.0,
+                in1=chan[:, 2 + side * (KW - 1), :],
+                op0=ALU.mult,
+                op1=ALU.mult,
+            )
+
+        def flip(raw, block):
+            words = raw[:].bitcast(F32)[:, block * (C // 2) : (block + 1) * (C // 2)]
+            flipped = turns.tile([P, PASSES, PAIRS, P], F32, tag="turn")
+            for g in range(PASSES):
+                for u in range(PAIRS):
+                    first = g * PAIRS * P + u
+                    last = (g + 1) * PAIRS * P
+                    nc.tensor.transpose(flipped[:, g, u, :], words[:, first:last:PAIRS], ident[:])
+            return flipped
+
+        def regroup(copy, flipped, grouped, rows, first_row):
+            words = grouped[:].bitcast(F32).rearrange("p (g r u) -> p g r u", g=PASSES, r=rows)
+            copy(out=words[:, :, first_row : first_row + P, :], in_=flipped[:].rearrange("p g u r -> p g r u"))
+
+        w_codes = consts.tile([P, D_TILES * PASSES * P], U32, align_bytes=64)
+        w_scales = consts.tile([P, D_TILES * PASSES * P], U8, align_bytes=64)
+        w_grouped = {}
+
+        def quantise_w(e):
+            cols = slice(e * PASSES * P, (e + 1) * PASSES * P)
+            nc.vector.quantize_mx(
+                out=w_codes[:, cols].bitcast(FP8X4), scales=w_scales[:, cols], in_=w_grouped[e][:]
+            )
+
+        x_grouped = {}
+        x_codes = {}
+        x_scales = {}
+
+        def quantise_x(bank_no):
+            x_codes[bank_no] = codes.tile([P, PASSES * BANK], U32, align_bytes=64, name="x_codes")
+            x_scales[bank_no] = codes.tile([P, PASSES * BANK], U8, align_bytes=64, name="x_scales")
+            nc.vector.quantize_mx(
+                out=x_codes[bank_no][:].bitcast(FP8X4), scales=x_scales[bank_no][:], in_=x_grouped[bank_no][:]
+            )
+
+        def multiply(b, e, h):
+            acc = accs.tile([P, BANK], F32)
+            bank_no = b * T_BANKS + h
+            for g in range(PASSES):
+                w_cols = slice((e * PASSES + g) * P, (e * PASSES + g + 1) * P)
+                x_cols = slice(g * BANK, (g + 1) * BANK)
+                nc.tensor.matmul_mx(
+                    out=acc[:],
+                    lhsT=w_codes[:, w_cols].bitcast(FP8X4),
+                    lhsT_scale=w_scales[:, w_cols],
+                    rhs=x_codes[bank_no][:, x_cols].bitcast(FP8X4),
+                    rhs_scale=x_scales[bank_no][:, x_cols],
+                    start=(g == 0),
+                    stop=(g == PASSES - 1),
+                )
+            return acc
+
+        def convolve(e, acc):
+            y = ys.tile([P, T], F32)
+            for h in range(T_BANKS):
+                nc.scalar.activation(
+                    out=y[:, h * BANK : (h + 1) * BANK],
+                    in_=acc[h][:],
+                    func=ACT.Identity,
+                    bias=bias_all[:, e : e + 1],
+                    scale=chan[:, 3, e : e + 1],
+                )
+            for j in (0, KW - 1):
+                shift = j - 1
+                for h in range(T_BANKS):
+                    src_lo = max(h * BANK, shift)
+                    src_hi = min((h + 1) * BANK, T + shift)
+                    nc.vector.scalar_tensor_tensor(
+                        out=y[:, src_lo - shift : src_hi - shift],
+                        in0=acc[h][:, src_lo - h * BANK : src_hi - h * BANK],
+                        scalar=chan[:, 2 + j, e : e + 1],
+                        in1=y[:, src_lo - shift : src_hi - shift],
+                        op0=ALU.mult,
+                        op1=ALU.add,
+                    )
+            nc.gpsimd.tensor_tensor(
+                out=y[:, 0 : T : T - 1], in0=y[:, 0 : T : T - 1], in1=edge_fix[:, e, :], op=ALU.add
+            )
+            return y
+
+        def turn_back(y, h):
+            back = turns.tile([P, BANK_BLOCKS, P], F32, tag="turn")
+            for i in range(BANK_BLOCKS):
+                k = h * BANK_BLOCKS + i
+                nc.tensor.transpose(back[:, i, :], y[:, k * P : (k + 1) * P], ident[:])
+            return back
+
+        y_rows = {}
+        out_rows = {}
+        for s in range(-X_AHEAD, STEPS + BACK_LAG):
+            n = s + X_AHEAD
+            e_next = s + W_AHEAD
+            done = s - BACK_LAG
+            multiplies = 0 <= s < STEPS
+            b, e = divmod(s, D_TILES)
+
+            if n % BANK_BLOCKS == 0 and 0 < n <= X_BLOCKS:
+                quantise_x(n // BANK_BLOCKS - 1)
+            if 0 < e_next <= D_TILES:
+                quantise_w(e_next - 1)
+
+            acc = []
+            back = []
+            if multiplies:
+                for h in range(T_BANKS):
+                    acc.append(multiply(b, e, h))
+            if done >= 0:
+                for h in range(T_BANKS):
+                    back.append(turn_back(y_rows[done], h))
+            if n < X_BLOCKS:
+                x_flipped = flip(x_raw, n)
+            if 0 <= e_next < D_TILES:
+                w_flipped = flip(w_raw, e_next)
+
+            if multiplies:
+                y_rows[s] = convolve(e, acc)
+            if done >= 0:
+                pair, j = divmod(done, STORE_TILES)
+                if j == 0:
+                    out_rows[pair] = outs.tile([P, T_BLOCKS, STORE_TILES * P], F32, name="out_rows")
+                for h in range(T_BANKS):
+                    copy = nc.vector.tensor_copy if (h == 1 and not multiplies) else nc.scalar.copy
+                    copy(
+                        out=out_rows[pair][:, h * BANK_BLOCKS : (h + 1) * BANK_BLOCKS, j * P : (j + 1) * P],
+                        in_=back[h][:],
+                    )
+                if j == STORE_TILES - 1:
+                    d_lo = (done % D_TILES - j) * P
+                    nc.sync.dma_start(
+                        out=out[done // D_TILES, :, d_lo : d_lo + STORE_TILES * P].rearrange(
+                            "(k p) d -> p k d", p=P
+                        ),
+                        in_=out_rows[pair][:],
+                    )
+            if n < X_BLOCKS:
+                bank_no, q = divmod(n, BANK_BLOCKS)
+                if q == 0:
+                    x_grouped[bank_no] = groups.tile(
+                        [P, PASSES * BANK * PACK], BF16, align_bytes=64, name="x_grouped"
+                    )
+                copy = nc.vector.tensor_copy if n % VECTOR_EVERY == VECTOR_EVERY - 1 else nc.scalar.copy
+                regroup(copy, x_flipped, x_grouped[bank_no], BANK, q * P)
+            if 0 <= e_next < D_TILES:
+                w_grouped[e_next] = groups.tile([P, PASSES * P * PACK], BF16, align_bytes=64, name="w_grouped")
+                regroup(nc.scalar.copy, w_flipped, w_grouped[e_next], P, 0)

@@ -27,10 +27,10 @@ LOAD_BLOCKS = 2
 STORE_TILES = 2
 
 STEPS = B * D_TILES
-X_AHEAD = T_BLOCKS + 1
+X_LEAD = 1
 W_AHEAD = 2
+WARM_UP = 12
 BACK_LAG = 3
-VECTOR_EVERY = 3
 
 FLOPS = 2 * B * T * C * D + 2 * KW * B * T * D
 
@@ -45,8 +45,8 @@ def tile_cvim_pa_t_kernel(tc, x, w1, b1, w2, b2, out):
         codes = pools.enter_context(tc.tile_pool(name="codes", bufs=2 * T_BANKS))
         ys = pools.enter_context(tc.tile_pool(name="ys", bufs=BACK_LAG + 2))
         outs = pools.enter_context(tc.tile_pool(name="outs", bufs=3))
-        accs = pools.enter_context(tc.psum_pool(name="accs", bufs=5))
-        turns = pools.enter_context(tc.psum_pool(name="turns", bufs=3))
+        accs = pools.enter_context(tc.psum_pool(name="accs", bufs=4))
+        turns = pools.enter_context(tc.psum_pool(name="turns", bufs=4))
 
         rows_bf16 = consts.tile([P, (2 + KW) * P], BF16)
         nc.gpsimd.memset(rows_bf16[:], 0.0)
@@ -67,12 +67,25 @@ def tile_cvim_pa_t_kernel(tc, x, w1, b1, w2, b2, out):
             )
 
         for first in range(0, T_BLOCKS, LOAD_BLOCKS):
+            if first == BANK_BLOCKS:
+                load_rows(w_raw, w1, 0)
             load_rows(x_raw, x_rows, first)
-        for first in range(0, D_TILES, LOAD_BLOCKS):
-            load_rows(w_raw, w1, first)
+        for first in range(0, T_BLOCKS, LOAD_BLOCKS):
+            if first + LOAD_BLOCKS < D_TILES:
+                load_rows(w_raw, w1, first + LOAD_BLOCKS)
             load_rows(x_raw, x_rows, T_BLOCKS + first)
         for first in range(2 * T_BLOCKS, X_BLOCKS, LOAD_BLOCKS):
             load_rows(x_raw, x_rows, first)
+
+        zeros = consts.tile([P, BANK], BF16)
+        nc.vector.memset(zeros[:], 0.0)
+
+        def keep_clock(count):
+            for k in range(count):
+                idle = accs.tile([P, BANK], F32, name="acc")
+                nc.tensor.matmul(idle[:], zeros[:, 0:P], zeros[:], start=True, stop=True)
+
+        keep_clock(WARM_UP)
 
         ident = consts.tile([P, P], F32)
         make_identity(nc, ident[:])
@@ -119,9 +132,9 @@ def tile_cvim_pa_t_kernel(tc, x, w1, b1, w2, b2, out):
                     nc.tensor.transpose(flipped[:, g, u, :], words[:, first:last:PAIRS], ident[:])
             return flipped
 
-        def regroup(copy, flipped, grouped, rows, first_row):
+        def regroup(flipped, grouped, rows, first_row):
             words = grouped[:].bitcast(F32).rearrange("p (g r u) -> p g r u", g=PASSES, r=rows)
-            copy(out=words[:, :, first_row : first_row + P, :], in_=flipped[:].rearrange("p g u r -> p g r u"))
+            nc.scalar.copy(out=words[:, :, first_row : first_row + P, :], in_=flipped[:].rearrange("p g u r -> p g r u"))
 
         w_codes = consts.tile([P, D_TILES * PASSES * P], U32, align_bytes=64)
         w_scales = consts.tile([P, D_TILES * PASSES * P], U8, align_bytes=64)
@@ -144,8 +157,21 @@ def tile_cvim_pa_t_kernel(tc, x, w1, b1, w2, b2, out):
                 out=x_codes[bank_no][:].bitcast(FP8X4), scales=x_scales[bank_no][:], in_=x_grouped[bank_no][:]
             )
 
+        def quantise_x_half(bank_no, half):
+            if half == 0:
+                x_codes[bank_no] = codes.tile([P, PASSES * BANK], U32, align_bytes=64, name="x_codes")
+                x_scales[bank_no] = codes.tile([P, PASSES * BANK], U8, align_bytes=64, name="x_scales")
+            for g in range(PASSES):
+                lo = g * BANK + half * (BANK // 2)
+                hi = lo + BANK // 2
+                nc.vector.quantize_mx(
+                    out=x_codes[bank_no][:, lo:hi].bitcast(FP8X4),
+                    scales=x_scales[bank_no][:, lo:hi],
+                    in_=x_grouped[bank_no][:, PACK * lo : PACK * hi],
+                )
+
         def multiply(b, e, h):
-            acc = accs.tile([P, BANK], F32)
+            acc = accs.tile([P, BANK], F32, name="acc")
             bank_no = b * T_BANKS + h
             for g in range(PASSES):
                 w_cols = slice((e * PASSES + g) * P, (e * PASSES + g + 1) * P)
@@ -196,18 +222,46 @@ def tile_cvim_pa_t_kernel(tc, x, w1, b1, w2, b2, out):
                 nc.tensor.transpose(back[:, i, :], y[:, k * P : (k + 1) * P], ident[:])
             return back
 
+        def take_x(n):
+            x_flipped = flip(x_raw, n)
+            bank_no, q = divmod(n, BANK_BLOCKS)
+            if q == 0:
+                x_grouped[bank_no] = groups.tile(
+                    [P, PASSES * BANK * PACK], BF16, align_bytes=64, name="x_grouped"
+                )
+            regroup(x_flipped, x_grouped[bank_no], BANK, q * P)
+
+        def take_w(e):
+            w_flipped = flip(w_raw, e)
+            w_grouped[e] = groups.tile([P, PASSES * P * PACK], BF16, align_bytes=64, name="w_grouped")
+            regroup(w_flipped, w_grouped[e], P, 0)
+
+        for n in range(T_BLOCKS):
+            if n == BANK_BLOCKS:
+                for e in range(W_AHEAD):
+                    take_w(e)
+                keep_clock(1)
+                quantise_x(0)
+                for e in range(W_AHEAD):
+                    quantise_w(e)
+            take_x(n)
+            if n % 2 == 1:
+                keep_clock(1)
+                if n > BANK_BLOCKS:
+                    quantise_x_half(1, (n - BANK_BLOCKS) // 2)
+
         y_rows = {}
         out_rows = {}
-        for s in range(-X_AHEAD, STEPS + BACK_LAG):
-            n = s + X_AHEAD
+        for s in range(STEPS + BACK_LAG):
+            n = T_BLOCKS + X_LEAD + s
             e_next = s + W_AHEAD
             done = s - BACK_LAG
-            multiplies = 0 <= s < STEPS
+            multiplies = s < STEPS
             b, e = divmod(s, D_TILES)
 
-            if n % BANK_BLOCKS == 0 and 0 < n <= X_BLOCKS:
+            if n % BANK_BLOCKS == X_LEAD - 1 and T_BLOCKS + X_LEAD < n < X_BLOCKS + X_LEAD:
                 quantise_x(n // BANK_BLOCKS - 1)
-            if 0 < e_next <= D_TILES:
+            if W_AHEAD < e_next <= D_TILES:
                 quantise_w(e_next - 1)
 
             acc = []
@@ -215,17 +269,10 @@ def tile_cvim_pa_t_kernel(tc, x, w1, b1, w2, b2, out):
             if multiplies:
                 for h in range(T_BANKS):
                     acc.append(multiply(b, e, h))
+                y_rows[s] = convolve(e, acc)
             if done >= 0:
                 for h in range(T_BANKS):
                     back.append(turn_back(y_rows[done], h))
-            if n < X_BLOCKS:
-                x_flipped = flip(x_raw, n)
-            if 0 <= e_next < D_TILES:
-                w_flipped = flip(w_raw, e_next)
-
-            if multiplies:
-                y_rows[s] = convolve(e, acc)
-            if done >= 0:
                 pair, j = divmod(done, STORE_TILES)
                 if j == 0:
                     out_rows[pair] = outs.tile([P, T_BLOCKS, STORE_TILES * P], F32, name="out_rows")
@@ -243,14 +290,7 @@ def tile_cvim_pa_t_kernel(tc, x, w1, b1, w2, b2, out):
                         ),
                         in_=out_rows[pair][:],
                     )
-            if n < X_BLOCKS:
-                bank_no, q = divmod(n, BANK_BLOCKS)
-                if q == 0:
-                    x_grouped[bank_no] = groups.tile(
-                        [P, PASSES * BANK * PACK], BF16, align_bytes=64, name="x_grouped"
-                    )
-                copy = nc.vector.tensor_copy if n % VECTOR_EVERY == VECTOR_EVERY - 1 else nc.scalar.copy
-                regroup(copy, x_flipped, x_grouped[bank_no], BANK, q * P)
-            if 0 <= e_next < D_TILES:
-                w_grouped[e_next] = groups.tile([P, PASSES * P * PACK], BF16, align_bytes=64, name="w_grouped")
-                regroup(nc.scalar.copy, w_flipped, w_grouped[e_next], P, 0)
+            for n in range(T_BLOCKS if s == 0 else n, min(n + 1, X_BLOCKS)):
+                take_x(n)
+            if e_next < D_TILES:
+                take_w(e_next)

@@ -28,8 +28,10 @@ STORE_TILES = 2
 
 STEPS = B * D_TILES
 X_LEAD = 1
-W_AHEAD = 2
-WARM_UP = 12
+W_AHEAD = 3
+VECTOR_EVERY = 8
+FINE_STEPS = 4
+WARM_UP = 9
 BACK_LAG = 3
 
 FLOPS = 2 * B * T * C * D + 2 * KW * B * T * D
@@ -49,10 +51,10 @@ def tile_cvim_pa_t_kernel(tc, x, w1, b1, w2, b2, out):
         turns = pools.enter_context(tc.psum_pool(name="turns", bufs=4))
 
         rows_bf16 = consts.tile([P, (2 + KW) * P], BF16)
-        nc.gpsimd.memset(rows_bf16[:], 0.0)
-        nc.sync.dma_start(out=rows_bf16[0:D_TILES, 0:P], in_=b1.rearrange("(e p) -> e p", p=P))
-        nc.sync.dma_start(out=rows_bf16[0:D_TILES, P : 2 * P], in_=b2.rearrange("(e p) -> e p", p=P))
-        nc.sync.dma_start(
+        nc.vector.memset(rows_bf16[:], 0.0)
+        nc.scalar.dma_start(out=rows_bf16[0:D_TILES, 0:P], in_=b1.rearrange("(e p) -> e p", p=P))
+        nc.scalar.dma_start(out=rows_bf16[0:D_TILES, P : 2 * P], in_=b2.rearrange("(e p) -> e p", p=P))
+        nc.scalar.dma_start(
             out=rows_bf16[0:D_TILES, 2 * P : (2 + KW) * P], in_=w2.rearrange("(e p) j -> e (p j)", p=P)
         )
 
@@ -60,13 +62,15 @@ def tile_cvim_pa_t_kernel(tc, x, w1, b1, w2, b2, out):
         x_raw = raws.tile([P, X_BLOCKS * C], BF16)
         w_raw = raws.tile([P, D_TILES * C], BF16)
 
-        def load_rows(raw, rows, first):
+        def load_rows(raw, rows, first, blocks=LOAD_BLOCKS):
             nc.sync.dma_start(
-                out=raw[:].rearrange("p (k c) -> p k c", c=C)[:, first : first + LOAD_BLOCKS, :],
-                in_=rows[first * P : (first + LOAD_BLOCKS) * P, :].rearrange("(k p) c -> p k c", p=P),
+                out=raw[:].rearrange("p (k c) -> p k c", c=C)[:, first : first + blocks, :],
+                in_=rows[first * P : (first + blocks) * P, :].rearrange("(k p) c -> p k c", p=P),
             )
 
-        for first in range(0, T_BLOCKS, LOAD_BLOCKS):
+        load_rows(x_raw, x_rows, 0, 1)
+        load_rows(x_raw, x_rows, 1, 1)
+        for first in range(LOAD_BLOCKS, T_BLOCKS, LOAD_BLOCKS):
             if first == BANK_BLOCKS:
                 load_rows(w_raw, w1, 0)
             load_rows(x_raw, x_rows, first)
@@ -90,37 +94,40 @@ def tile_cvim_pa_t_kernel(tc, x, w1, b1, w2, b2, out):
         ident = consts.tile([P, P], F32)
         make_identity(nc, ident[:])
 
-        rows_f32 = consts.tile([P, 2 + KW, P], F32)
-        nc.vector.tensor_copy(
-            out=rows_f32[:, 0:2, :], in_=rows_bf16[:, 0 : 2 * P].rearrange("e (v p) -> e v p", v=2)
-        )
-        nc.vector.tensor_copy(
-            out=rows_f32[:, 2 : 2 + KW, :],
-            in_=rows_bf16[:, 2 * P : (2 + KW) * P].rearrange("e (p j) -> e j p", j=KW),
-        )
         chan = consts.tile([P, 2 + KW, D_TILES], F32)
-        for v in range(2 + KW):
-            column = turns.tile([P, P], F32, tag="turn")
-            nc.tensor.transpose(column[:], rows_f32[:, v, :], ident[:])
-            nc.vector.tensor_copy(out=chan[:, v, :], in_=column[:, 0:D_TILES])
-        bias1 = chan[:, 0, :]
-        bias2 = chan[:, 1, :]
-        tap_sum = consts.tile([P, D_TILES], F32)
-        nc.vector.tensor_tensor(out=tap_sum[:], in0=chan[:, 2, :], in1=chan[:, 3, :], op=ALU.add)
-        nc.vector.tensor_tensor(out=tap_sum[:], in0=tap_sum[:], in1=chan[:, 4, :], op=ALU.add)
         bias_all = consts.tile([P, D_TILES], F32)
-        nc.vector.tensor_tensor(out=bias_all[:], in0=tap_sum[:], in1=bias1, op=ALU.mult)
-        nc.vector.tensor_tensor(out=bias_all[:], in0=bias_all[:], in1=bias2, op=ALU.add)
         edge_fix = consts.tile([P, D_TILES, 2], F32)
-        for side in range(2):
-            nc.vector.scalar_tensor_tensor(
-                out=edge_fix[:, :, side],
-                in0=bias1,
-                scalar=-1.0,
-                in1=chan[:, 2 + side * (KW - 1), :],
-                op0=ALU.mult,
-                op1=ALU.mult,
+
+        def prepare_channels():
+            rows_f32 = consts.tile([P, 2 + KW, P], F32)
+            nc.vector.tensor_copy(
+                out=rows_f32[:, 0:2, :], in_=rows_bf16[:, 0 : 2 * P].rearrange("e (v p) -> e v p", v=2)
             )
+            nc.vector.tensor_copy(
+                out=rows_f32[:, 2 : 2 + KW, :],
+                in_=rows_bf16[:, 2 * P : (2 + KW) * P].rearrange("e (p j) -> e j p", j=KW),
+            )
+            for v in range(2 + KW):
+                column = turns.tile([P, P], F32, tag="turn")
+                nc.tensor.transpose(column[:], rows_f32[:, v, :], ident[:])
+                nc.vector.tensor_copy(out=chan[:, v, :], in_=column[:, 0:D_TILES])
+            bias1 = chan[:, 0, :]
+            bias2 = chan[:, 1, :]
+            tap_sum = consts.tile([P, D_TILES], F32)
+            nc.vector.tensor_tensor(out=tap_sum[:], in0=chan[:, 2, :], in1=chan[:, 3, :], op=ALU.add)
+            nc.vector.tensor_tensor(out=tap_sum[:], in0=tap_sum[:], in1=chan[:, 4, :], op=ALU.add)
+            nc.vector.tensor_tensor(out=bias_all[:], in0=tap_sum[:], in1=bias1, op=ALU.mult)
+            nc.vector.tensor_tensor(out=bias_all[:], in0=bias_all[:], in1=bias2, op=ALU.add)
+            for side in range(2):
+                nc.vector.scalar_tensor_tensor(
+                    out=edge_fix[:, :, side],
+                    in0=bias1,
+                    scalar=-1.0,
+                    in1=chan[:, 2 + side * (KW - 1), :],
+                    op0=ALU.mult,
+                    op1=ALU.mult,
+                )
+
 
         def flip(raw, block):
             words = raw[:].bitcast(F32)[:, block * (C // 2) : (block + 1) * (C // 2)]
@@ -132,9 +139,9 @@ def tile_cvim_pa_t_kernel(tc, x, w1, b1, w2, b2, out):
                     nc.tensor.transpose(flipped[:, g, u, :], words[:, first:last:PAIRS], ident[:])
             return flipped
 
-        def regroup(flipped, grouped, rows, first_row):
+        def regroup(copy, flipped, grouped, rows, first_row):
             words = grouped[:].bitcast(F32).rearrange("p (g r u) -> p g r u", g=PASSES, r=rows)
-            nc.scalar.copy(out=words[:, :, first_row : first_row + P, :], in_=flipped[:].rearrange("p g u r -> p g r u"))
+            copy(out=words[:, :, first_row : first_row + P, :], in_=flipped[:].rearrange("p g u r -> p g r u"))
 
         w_codes = consts.tile([P, D_TILES * PASSES * P], U32, align_bytes=64)
         w_scales = consts.tile([P, D_TILES * PASSES * P], U8, align_bytes=64)
@@ -150,24 +157,17 @@ def tile_cvim_pa_t_kernel(tc, x, w1, b1, w2, b2, out):
         x_codes = {}
         x_scales = {}
 
-        def quantise_x(bank_no):
-            x_codes[bank_no] = codes.tile([P, PASSES * BANK], U32, align_bytes=64, name="x_codes")
-            x_scales[bank_no] = codes.tile([P, PASSES * BANK], U8, align_bytes=64, name="x_scales")
-            nc.vector.quantize_mx(
-                out=x_codes[bank_no][:].bitcast(FP8X4), scales=x_scales[bank_no][:], in_=x_grouped[bank_no][:]
-            )
-
-        def quantise_x_half(bank_no, half):
-            if half == 0:
+        def quantise_x(n):
+            bank_no, q = divmod(n, BANK_BLOCKS)
+            if bank_no not in x_codes:
                 x_codes[bank_no] = codes.tile([P, PASSES * BANK], U32, align_bytes=64, name="x_codes")
                 x_scales[bank_no] = codes.tile([P, PASSES * BANK], U8, align_bytes=64, name="x_scales")
             for g in range(PASSES):
-                lo = g * BANK + half * (BANK // 2)
-                hi = lo + BANK // 2
+                cols = slice(g * BANK + (q - 1) * P, g * BANK + (q + 1) * P)
                 nc.vector.quantize_mx(
-                    out=x_codes[bank_no][:, lo:hi].bitcast(FP8X4),
-                    scales=x_scales[bank_no][:, lo:hi],
-                    in_=x_grouped[bank_no][:, PACK * lo : PACK * hi],
+                    out=x_codes[bank_no][:, cols].bitcast(FP8X4),
+                    scales=x_scales[bank_no][:, cols],
+                    in_=x_grouped[bank_no][:, PACK * cols.start : PACK * cols.stop],
                 )
 
         def multiply(b, e, h):
@@ -187,16 +187,16 @@ def tile_cvim_pa_t_kernel(tc, x, w1, b1, w2, b2, out):
                 )
             return acc
 
-        def convolve(e, acc):
-            y = ys.tile([P, T], F32)
-            for h in range(T_BANKS):
-                nc.scalar.activation(
-                    out=y[:, h * BANK : (h + 1) * BANK],
-                    in_=acc[h][:],
-                    func=ACT.Identity,
-                    bias=bias_all[:, e : e + 1],
-                    scale=chan[:, 3, e : e + 1],
-                )
+        def middle_tap(e, y, acc, h):
+            nc.scalar.activation(
+                out=y[:, h * BANK : (h + 1) * BANK],
+                in_=acc[h][:],
+                func=ACT.Identity,
+                bias=bias_all[:, e : e + 1],
+                scale=chan[:, 3, e : e + 1],
+            )
+
+        def outer_taps(e, y, acc):
             for j in (0, KW - 1):
                 shift = j - 1
                 for h in range(T_BANKS):
@@ -213,7 +213,12 @@ def tile_cvim_pa_t_kernel(tc, x, w1, b1, w2, b2, out):
             nc.gpsimd.tensor_tensor(
                 out=y[:, 0 : T : T - 1], in0=y[:, 0 : T : T - 1], in1=edge_fix[:, e, :], op=ALU.add
             )
-            return y
+
+        def store(b, t_lo, t_hi, d_lo, width, rows, col):
+            nc.sync.dma_start(
+                out=out[b, t_lo:t_hi, d_lo : d_lo + width].rearrange("(k p) d -> p k d", p=P),
+                in_=rows[:, t_lo // P : t_hi // P, col : col + width],
+            )
 
         def turn_back(y, h):
             back = turns.tile([P, BANK_BLOCKS, P], F32, tag="turn")
@@ -222,57 +227,73 @@ def tile_cvim_pa_t_kernel(tc, x, w1, b1, w2, b2, out):
                 nc.tensor.transpose(back[:, i, :], y[:, k * P : (k + 1) * P], ident[:])
             return back
 
-        def take_x(n):
+        def take_x(n, copy=nc.scalar.copy):
             x_flipped = flip(x_raw, n)
             bank_no, q = divmod(n, BANK_BLOCKS)
             if q == 0:
                 x_grouped[bank_no] = groups.tile(
                     [P, PASSES * BANK * PACK], BF16, align_bytes=64, name="x_grouped"
                 )
-            regroup(x_flipped, x_grouped[bank_no], BANK, q * P)
+            regroup(copy, x_flipped, x_grouped[bank_no], BANK, q * P)
 
         def take_w(e):
             w_flipped = flip(w_raw, e)
             w_grouped[e] = groups.tile([P, PASSES * P * PACK], BF16, align_bytes=64, name="w_grouped")
-            regroup(w_flipped, w_grouped[e], P, 0)
+            regroup(nc.scalar.copy, w_flipped, w_grouped[e], P, 0)
 
-        for n in range(T_BLOCKS):
-            if n == BANK_BLOCKS:
-                for e in range(W_AHEAD):
-                    take_w(e)
-                keep_clock(1)
-                quantise_x(0)
-                for e in range(W_AHEAD):
-                    quantise_w(e)
-            take_x(n)
-            if n % 2 == 1:
-                keep_clock(1)
-                if n > BANK_BLOCKS:
-                    quantise_x_half(1, (n - BANK_BLOCKS) // 2)
+        take_x(0)
+        take_x(1)
+        prepare_channels()
+        keep_clock(1)
+        quantise_x(1)
+        take_x(2)
+        take_x(3)
+        keep_clock(1)
+        quantise_x(3)
+        take_w(0)
+        quantise_w(0)
+        take_x(4)
+        take_x(5)
+        quantise_x(5)
+        take_x(6)
+        y_rows = {0: ys.tile([P, T], F32, name="y")}
+        acc = [multiply(0, 0, 0)]
+        middle_tap(0, y_rows[0], acc, 0)
+        take_x(7)
+        take_w(1)
+        keep_clock(1)
+        quantise_x(7)
+        quantise_w(1)
+        take_w(2)
+        take_x(8)
+        quantise_w(2)
+        acc.append(multiply(0, 0, 1))
+        middle_tap(0, y_rows[0], acc, 1)
+        outer_taps(0, y_rows[0], acc)
+        take_w(3)
+        take_x(9)
 
-        y_rows = {}
         out_rows = {}
-        for s in range(STEPS + BACK_LAG):
+        for s in range(1, STEPS + BACK_LAG):
             n = T_BLOCKS + X_LEAD + s
             e_next = s + W_AHEAD
             done = s - BACK_LAG
             multiplies = s < STEPS
             b, e = divmod(s, D_TILES)
 
-            if n % BANK_BLOCKS == X_LEAD - 1 and T_BLOCKS + X_LEAD < n < X_BLOCKS + X_LEAD:
-                quantise_x(n // BANK_BLOCKS - 1)
-            if W_AHEAD < e_next <= D_TILES:
+            if n % 2 == 0 and n - 1 < X_BLOCKS:
+                quantise_x(n - 1)
+            if e_next - 1 < D_TILES:
                 quantise_w(e_next - 1)
 
-            acc = []
-            back = []
             if multiplies:
+                acc = [multiply(b, e, h) for h in range(T_BANKS)]
+                y_rows[s] = ys.tile([P, T], F32, name="y")
                 for h in range(T_BANKS):
-                    acc.append(multiply(b, e, h))
-                y_rows[s] = convolve(e, acc)
+                    middle_tap(e, y_rows[s], acc, h)
+                outer_taps(e, y_rows[s], acc)
             if done >= 0:
-                for h in range(T_BANKS):
-                    back.append(turn_back(y_rows[done], h))
+                back = [turn_back(y_rows[done], h) for h in range(T_BANKS)]
                 pair, j = divmod(done, STORE_TILES)
                 if j == 0:
                     out_rows[pair] = outs.tile([P, T_BLOCKS, STORE_TILES * P], F32, name="out_rows")
@@ -282,15 +303,11 @@ def tile_cvim_pa_t_kernel(tc, x, w1, b1, w2, b2, out):
                         out=out_rows[pair][:, h * BANK_BLOCKS : (h + 1) * BANK_BLOCKS, j * P : (j + 1) * P],
                         in_=back[h][:],
                     )
-                if j == STORE_TILES - 1:
-                    d_lo = (done % D_TILES - j) * P
-                    nc.sync.dma_start(
-                        out=out[done // D_TILES, :, d_lo : d_lo + STORE_TILES * P].rearrange(
-                            "(k p) d -> p k d", p=P
-                        ),
-                        in_=out_rows[pair][:],
-                    )
-            for n in range(T_BLOCKS if s == 0 else n, min(n + 1, X_BLOCKS)):
-                take_x(n)
+                    if done >= STEPS - FINE_STEPS:
+                        store(done // D_TILES, h * BANK, (h + 1) * BANK, done % D_TILES * P, P, out_rows[pair], j * P)
+                if j == STORE_TILES - 1 and done < STEPS - FINE_STEPS:
+                    store(done // D_TILES, 0, T, (done % D_TILES - j) * P, STORE_TILES * P, out_rows[pair], 0)
+            if n < X_BLOCKS:
+                take_x(n, nc.vector.tensor_copy if n % VECTOR_EVERY == 2 else nc.scalar.copy)
             if e_next < D_TILES:
                 take_w(e_next)

@@ -23,13 +23,14 @@ T_BLOCKS = T // P
 X_BLOCKS = B * T_BLOCKS
 BANK_BLOCKS = BANK // P
 D_TILES = D // P
+B2_ROW, W2_ROW = D_TILES, 2 * D_TILES
 LOAD_BLOCKS = 2
 STORE_TILES = 2
 
 STEPS = B * D_TILES
 X_LEAD = 1
 W_AHEAD = 3
-VECTOR_EVERY = 8
+VECTOR_EVERY = 6
 FINE_STEPS = 4
 WARM_UP = 9
 BACK_LAG = 3
@@ -50,13 +51,13 @@ def tile_cvim_pa_t_kernel(tc, x, w1, b1, w2, b2, out):
         accs = pools.enter_context(tc.psum_pool(name="accs", bufs=4))
         turns = pools.enter_context(tc.psum_pool(name="turns", bufs=4))
 
-        rows_bf16 = consts.tile([P, (2 + KW) * P], BF16)
-        nc.vector.memset(rows_bf16[:], 0.0)
-        nc.scalar.dma_start(out=rows_bf16[0:D_TILES, 0:P], in_=b1.rearrange("(e p) -> e p", p=P))
-        nc.scalar.dma_start(out=rows_bf16[0:D_TILES, P : 2 * P], in_=b2.rearrange("(e p) -> e p", p=P))
-        nc.scalar.dma_start(
-            out=rows_bf16[0:D_TILES, 2 * P : (2 + KW) * P], in_=w2.rearrange("(e p) j -> e (p j)", p=P)
-        )
+        zeros = consts.tile([P, BANK], BF16)
+        nc.vector.memset(zeros[:], 0.0)
+        rows = consts.tile([P, KW * P], BF16)
+        nc.gpsimd.memset(rows[:], 0.0)
+        nc.scalar.dma_start(out=rows[0:B2_ROW, 0:P], in_=b1.rearrange("(e p) -> e p", p=P))
+        nc.scalar.dma_start(out=rows[B2_ROW:W2_ROW, 0:P], in_=b2.rearrange("(e p) -> e p", p=P))
+        nc.scalar.dma_start(out=rows[W2_ROW : W2_ROW + D_TILES, :], in_=w2.rearrange("(e p) j -> e (p j)", p=P))
 
         x_rows = x.flatten_outer_dims()
         x_raw = raws.tile([P, X_BLOCKS * C], BF16)
@@ -81,9 +82,6 @@ def tile_cvim_pa_t_kernel(tc, x, w1, b1, w2, b2, out):
         for first in range(2 * T_BLOCKS, X_BLOCKS, LOAD_BLOCKS):
             load_rows(x_raw, x_rows, first)
 
-        zeros = consts.tile([P, BANK], BF16)
-        nc.vector.memset(zeros[:], 0.0)
-
         def keep_clock(count):
             for k in range(count):
                 idle = accs.tile([P, BANK], F32, name="acc")
@@ -94,41 +92,32 @@ def tile_cvim_pa_t_kernel(tc, x, w1, b1, w2, b2, out):
         ident = consts.tile([P, P], F32)
         make_identity(nc, ident[:])
 
-        chan = consts.tile([P, 2 + KW, D_TILES], F32)
+        ident_bf16 = consts.tile([P, P], BF16)
+        nc.gpsimd.tensor_copy(out=ident_bf16[:], in_=ident[:])
+
+        bias = consts.tile([P, 2, D_TILES], F32)
+        taps = consts.tile([P, KW, D_TILES], F32)
         bias_all = consts.tile([P, D_TILES], F32)
-        edge_fix = consts.tile([P, D_TILES, 2], F32)
+        edge = consts.tile([P, D_TILES, 2], F32)
 
         def prepare_channels():
-            rows_f32 = consts.tile([P, 2 + KW, P], F32)
+            columns = turns.tile([P, 1 + KW, P], BF16, tag="turn")
+            nc.tensor.transpose(columns[:, 0, :], rows[:, 0:P], ident_bf16[:])
+            for j in range(KW):
+                nc.tensor.transpose(columns[:, 1 + j, :], rows[:, j : KW * P : KW], ident_bf16[:])
             nc.vector.tensor_copy(
-                out=rows_f32[:, 0:2, :], in_=rows_bf16[:, 0 : 2 * P].rearrange("e (v p) -> e v p", v=2)
+                out=bias[:], in_=columns[:, 0, 0:W2_ROW].rearrange("p (v e) -> p v e", v=2)
             )
-            nc.vector.tensor_copy(
-                out=rows_f32[:, 2 : 2 + KW, :],
-                in_=rows_bf16[:, 2 * P : (2 + KW) * P].rearrange("e (p j) -> e j p", j=KW),
-            )
-            for v in range(2 + KW):
-                column = turns.tile([P, P], F32, tag="turn")
-                nc.tensor.transpose(column[:], rows_f32[:, v, :], ident[:])
-                nc.vector.tensor_copy(out=chan[:, v, :], in_=column[:, 0:D_TILES])
-            bias1 = chan[:, 0, :]
-            bias2 = chan[:, 1, :]
+            nc.vector.tensor_copy(out=taps[:], in_=columns[:, 1 : 1 + KW, W2_ROW : W2_ROW + D_TILES])
             tap_sum = consts.tile([P, D_TILES], F32)
-            nc.vector.tensor_tensor(out=tap_sum[:], in0=chan[:, 2, :], in1=chan[:, 3, :], op=ALU.add)
-            nc.vector.tensor_tensor(out=tap_sum[:], in0=tap_sum[:], in1=chan[:, 4, :], op=ALU.add)
-            nc.vector.tensor_tensor(out=bias_all[:], in0=tap_sum[:], in1=bias1, op=ALU.mult)
-            nc.vector.tensor_tensor(out=bias_all[:], in0=bias_all[:], in1=bias2, op=ALU.add)
+            nc.gpsimd.tensor_tensor(out=tap_sum[:], in0=taps[:, 0, :], in1=taps[:, 1, :], op=ALU.add)
+            nc.gpsimd.tensor_tensor(out=tap_sum[:], in0=tap_sum[:], in1=taps[:, 2, :], op=ALU.add)
+            nc.gpsimd.tensor_tensor(out=bias_all[:], in0=tap_sum[:], in1=bias[:, 0, :], op=ALU.mult)
+            nc.gpsimd.tensor_tensor(out=bias_all[:], in0=bias_all[:], in1=bias[:, 1, :], op=ALU.add)
             for side in range(2):
-                nc.vector.scalar_tensor_tensor(
-                    out=edge_fix[:, :, side],
-                    in0=bias1,
-                    scalar=-1.0,
-                    in1=chan[:, 2 + side * (KW - 1), :],
-                    op0=ALU.mult,
-                    op1=ALU.mult,
+                nc.gpsimd.tensor_tensor(
+                    out=edge[:, :, side], in0=bias[:, 0, :], in1=taps[:, side * (KW - 1), :], op=ALU.mult
                 )
-
-
         def flip(raw, block):
             words = raw[:].bitcast(F32)[:, block * (C // 2) : (block + 1) * (C // 2)]
             flipped = turns.tile([P, PASSES, PAIRS, P], F32, tag="turn")
@@ -193,7 +182,7 @@ def tile_cvim_pa_t_kernel(tc, x, w1, b1, w2, b2, out):
                 in_=acc[h][:],
                 func=ACT.Identity,
                 bias=bias_all[:, e : e + 1],
-                scale=chan[:, 3, e : e + 1],
+                scale=taps[:, 1, e : e + 1],
             )
 
         def outer_taps(e, y, acc):
@@ -205,13 +194,13 @@ def tile_cvim_pa_t_kernel(tc, x, w1, b1, w2, b2, out):
                     nc.vector.scalar_tensor_tensor(
                         out=y[:, src_lo - shift : src_hi - shift],
                         in0=acc[h][:, src_lo - h * BANK : src_hi - h * BANK],
-                        scalar=chan[:, 2 + j, e : e + 1],
+                        scalar=taps[:, j, e : e + 1],
                         in1=y[:, src_lo - shift : src_hi - shift],
                         op0=ALU.mult,
                         op1=ALU.add,
                     )
             nc.gpsimd.tensor_tensor(
-                out=y[:, 0 : T : T - 1], in0=y[:, 0 : T : T - 1], in1=edge_fix[:, e, :], op=ALU.add
+                out=y[:, 0 : T : T - 1], in0=y[:, 0 : T : T - 1], in1=edge[:, e, :], op=ALU.subtract
             )
 
         def store(b, t_lo, t_hi, d_lo, width, rows, col):
@@ -243,11 +232,11 @@ def tile_cvim_pa_t_kernel(tc, x, w1, b1, w2, b2, out):
 
         take_x(0)
         take_x(1)
-        prepare_channels()
         keep_clock(1)
         quantise_x(1)
         take_x(2)
         take_x(3)
+        prepare_channels()
         keep_clock(1)
         quantise_x(3)
         take_w(0)

@@ -32,7 +32,7 @@ X_LEAD = 1
 W_AHEAD = 3
 VECTOR_EVERY = 6
 FINE_STEPS = 4
-WARM_UP = 9
+WARM_UP = 7
 BACK_LAG = 3
 
 FLOPS = 2 * B * T * C * D + 2 * KW * B * T * D
@@ -185,20 +185,20 @@ def tile_cvim_pa_t_kernel(tc, x, w1, b1, w2, b2, out):
                 scale=taps[:, 1, e : e + 1],
             )
 
-        def outer_taps(e, y, acc):
-            for j in (0, KW - 1):
-                shift = j - 1
-                for h in range(T_BANKS):
-                    src_lo = max(h * BANK, shift)
-                    src_hi = min((h + 1) * BANK, T + shift)
-                    nc.vector.scalar_tensor_tensor(
-                        out=y[:, src_lo - shift : src_hi - shift],
-                        in0=acc[h][:, src_lo - h * BANK : src_hi - h * BANK],
-                        scalar=taps[:, j, e : e + 1],
-                        in1=y[:, src_lo - shift : src_hi - shift],
-                        op0=ALU.mult,
-                        op1=ALU.add,
-                    )
+        def outer_tap(e, y, acc, j, h, lo=0, hi=BANK):
+            to = h * BANK + 1 - j
+            lo = max(lo, -to)
+            hi = min(hi, T - to)
+            nc.vector.scalar_tensor_tensor(
+                out=y[:, to + lo : to + hi],
+                in0=acc[h][:, lo:hi],
+                scalar=taps[:, j, e : e + 1],
+                in1=y[:, to + lo : to + hi],
+                op0=ALU.mult,
+                op1=ALU.add,
+            )
+
+        def fix_ends(e, y):
             nc.gpsimd.tensor_tensor(
                 out=y[:, 0 : T : T - 1], in0=y[:, 0 : T : T - 1], in1=edge[:, e, :], op=ALU.subtract
             )
@@ -251,14 +251,19 @@ def tile_cvim_pa_t_kernel(tc, x, w1, b1, w2, b2, out):
         take_x(7)
         take_w(1)
         keep_clock(1)
+        outer_tap(0, y_rows[0], acc, 0, 0, hi=BANK - 1)
         quantise_x(7)
         quantise_w(1)
+        outer_tap(0, y_rows[0], acc, 2, 0)
         take_w(2)
         take_x(8)
         quantise_w(2)
         acc.append(multiply(0, 0, 1))
         middle_tap(0, y_rows[0], acc, 1)
-        outer_taps(0, y_rows[0], acc)
+        outer_tap(0, y_rows[0], acc, 0, 0, lo=BANK - 1)
+        outer_tap(0, y_rows[0], acc, 0, 1)
+        outer_tap(0, y_rows[0], acc, 2, 1)
+        fix_ends(0, y_rows[0])
         take_w(3)
         take_x(9)
 
@@ -280,14 +285,17 @@ def tile_cvim_pa_t_kernel(tc, x, w1, b1, w2, b2, out):
                 y_rows[s] = ys.tile([P, T], F32, name="y")
                 for h in range(T_BANKS):
                     middle_tap(e, y_rows[s], acc, h)
-                outer_taps(e, y_rows[s], acc)
+                for j in (0, KW - 1):
+                    for h in range(T_BANKS):
+                        outer_tap(e, y_rows[s], acc, j, h)
+                fix_ends(e, y_rows[s])
             if done >= 0:
                 back = [turn_back(y_rows[done], h) for h in range(T_BANKS)]
                 pair, j = divmod(done, STORE_TILES)
                 if j == 0:
                     out_rows[pair] = outs.tile([P, T_BLOCKS, STORE_TILES * P], F32, name="out_rows")
                 for h in range(T_BANKS):
-                    copy = nc.vector.tensor_copy if (h == 1 and not multiplies) else nc.scalar.copy
+                    copy = nc.vector.tensor_copy if (h == 1 and s > STEPS) else nc.scalar.copy
                     copy(
                         out=out_rows[pair][:, h * BANK_BLOCKS : (h + 1) * BANK_BLOCKS, j * P : (j + 1) * P],
                         in_=back[h][:],

@@ -21,6 +21,7 @@ BANK = 512
 T_BANKS = T // BANK
 T_BLOCKS = T // P
 X_BLOCKS = B * T_BLOCKS
+PAIR_BLOCKS = 2
 BANK_BLOCKS = BANK // P
 D_TILES = D // P
 B2_ROW, W2_ROW = D_TILES, 2 * D_TILES
@@ -44,10 +45,10 @@ def tile_cvim_pa_t_kernel(tc, x, w1, b1, w2, b2, out):
         pools.enter_context(tc.manual_schedule())
         consts = pools.enter_context(tc.tile_pool(name="consts", bufs=1))
         raws = pools.enter_context(tc.tile_pool(name="raws", bufs=1))
-        groups = pools.enter_context(tc.tile_pool(name="groups", bufs=2))
+        wides = pools.enter_context(tc.tile_pool(name="wides", bufs=16))
+        groups = pools.enter_context(tc.tile_pool(name="groups", bufs=4))
         codes = pools.enter_context(tc.tile_pool(name="codes", bufs=2 * T_BANKS))
         ys = pools.enter_context(tc.tile_pool(name="ys", bufs=BACK_LAG + 2))
-        outs = pools.enter_context(tc.tile_pool(name="outs", bufs=3))
         accs = pools.enter_context(tc.psum_pool(name="accs", bufs=4))
         turns = pools.enter_context(tc.psum_pool(name="turns", bufs=4))
 
@@ -60,27 +61,30 @@ def tile_cvim_pa_t_kernel(tc, x, w1, b1, w2, b2, out):
         nc.scalar.dma_start(out=rows[W2_ROW : W2_ROW + D_TILES, :], in_=w2.rearrange("(e p) j -> e (p j)", p=P))
 
         x_rows = x.flatten_outer_dims()
-        x_raw = raws.tile([P, X_BLOCKS * C], BF16)
+        x_raw = [wides.tile([P, BANK_BLOCKS * C], BF16, name="wide") for k in range(X_BLOCKS // BANK_BLOCKS)]
         w_raw = raws.tile([P, D_TILES * C], BF16)
 
-        def load_rows(raw, rows, first, blocks=LOAD_BLOCKS):
+        def load_rows(raw, k, rows, first, blocks=LOAD_BLOCKS):
             nc.sync.dma_start(
-                out=raw[:].rearrange("p (k c) -> p k c", c=C)[:, first : first + blocks, :],
+                out=raw[:].rearrange("p (k c) -> p k c", c=C)[:, k : k + blocks, :],
                 in_=rows[first * P : (first + blocks) * P, :].rearrange("(k p) c -> p k c", p=P),
             )
 
-        load_rows(x_raw, x_rows, 0, 1)
-        load_rows(x_raw, x_rows, 1, 1)
+        def load_x(first, blocks=LOAD_BLOCKS):
+            load_rows(x_raw[first // BANK_BLOCKS], first % BANK_BLOCKS, x_rows, first, blocks)
+
+        load_x(0, 1)
+        load_x(1, 1)
         for first in range(LOAD_BLOCKS, T_BLOCKS, LOAD_BLOCKS):
             if first == BANK_BLOCKS:
-                load_rows(w_raw, w1, 0)
-            load_rows(x_raw, x_rows, first)
+                load_rows(w_raw, 0, w1, 0)
+            load_x(first)
         for first in range(0, T_BLOCKS, LOAD_BLOCKS):
             if first + LOAD_BLOCKS < D_TILES:
-                load_rows(w_raw, w1, first + LOAD_BLOCKS)
-            load_rows(x_raw, x_rows, T_BLOCKS + first)
+                load_rows(w_raw, first + LOAD_BLOCKS, w1, first + LOAD_BLOCKS)
+            load_x(T_BLOCKS + first)
         for first in range(2 * T_BLOCKS, X_BLOCKS, LOAD_BLOCKS):
-            load_rows(x_raw, x_rows, first)
+            load_x(first)
 
         def keep_clock(count):
             for k in range(count):
@@ -128,8 +132,8 @@ def tile_cvim_pa_t_kernel(tc, x, w1, b1, w2, b2, out):
                     nc.tensor.transpose(flipped[:, g, u, :], words[:, first:last:PAIRS], ident[:])
             return flipped
 
-        def regroup(copy, flipped, grouped, rows, first_row):
-            words = grouped[:].bitcast(F32).rearrange("p (g r u) -> p g r u", g=PASSES, r=rows)
+        def regroup(copy, flipped, grouped, n_rows, first_row):
+            words = grouped[:].bitcast(F32).rearrange("p (g r u) -> p g r u", g=PASSES, r=n_rows)
             copy(out=words[:, :, first_row : first_row + P, :], in_=flipped[:].rearrange("p g u r -> p g r u"))
 
         w_codes = consts.tile([P, D_TILES * PASSES * P], U32, align_bytes=64)
@@ -151,12 +155,13 @@ def tile_cvim_pa_t_kernel(tc, x, w1, b1, w2, b2, out):
             if bank_no not in x_codes:
                 x_codes[bank_no] = codes.tile([P, PASSES * BANK], U32, align_bytes=64, name="x_codes")
                 x_scales[bank_no] = codes.tile([P, PASSES * BANK], U8, align_bytes=64, name="x_scales")
+            width = PAIR_BLOCKS * P
             for g in range(PASSES):
                 cols = slice(g * BANK + (q - 1) * P, g * BANK + (q + 1) * P)
                 nc.vector.quantize_mx(
                     out=x_codes[bank_no][:, cols].bitcast(FP8X4),
                     scales=x_scales[bank_no][:, cols],
-                    in_=x_grouped[bank_no][:, PACK * cols.start : PACK * cols.stop],
+                    in_=x_grouped[n // PAIR_BLOCKS][:, g * width * PACK : (g + 1) * width * PACK],
                 )
 
         def multiply(b, e, h):
@@ -217,13 +222,13 @@ def tile_cvim_pa_t_kernel(tc, x, w1, b1, w2, b2, out):
             return back
 
         def take_x(n, copy=nc.scalar.copy):
-            x_flipped = flip(x_raw, n)
-            bank_no, q = divmod(n, BANK_BLOCKS)
+            x_flipped = flip(x_raw[n // BANK_BLOCKS], n % BANK_BLOCKS)
+            pair, q = divmod(n, PAIR_BLOCKS)
             if q == 0:
-                x_grouped[bank_no] = groups.tile(
-                    [P, PASSES * BANK * PACK], BF16, align_bytes=64, name="x_grouped"
+                x_grouped[pair] = groups.tile(
+                    [P, PASSES * PAIR_BLOCKS * P * PACK], BF16, align_bytes=64, name="x_grouped"
                 )
-            regroup(copy, x_flipped, x_grouped[bank_no], BANK, q * P)
+            regroup(copy, x_flipped, x_grouped[pair], PAIR_BLOCKS * P, q * P)
 
         def take_w(e):
             w_flipped = flip(w_raw, e)
@@ -293,7 +298,7 @@ def tile_cvim_pa_t_kernel(tc, x, w1, b1, w2, b2, out):
                 back = [turn_back(y_rows[done], h) for h in range(T_BANKS)]
                 pair, j = divmod(done, STORE_TILES)
                 if j == 0:
-                    out_rows[pair] = outs.tile([P, T_BLOCKS, STORE_TILES * P], F32, name="out_rows")
+                    out_rows[pair] = wides.tile([P, T_BLOCKS, STORE_TILES * P], F32, name="wide")
                 for h in range(T_BANKS):
                     copy = nc.vector.tensor_copy if (h == 1 and s > STEPS) else nc.scalar.copy
                     copy(

@@ -32,7 +32,7 @@ STEPS = B * D_TILES
 X_LEAD = 1
 W_AHEAD = 3
 VECTOR_EVERY = 6
-FINE_STEPS = 4
+FINE_STEPS = 8
 WARM_UP = 7
 BACK_LAG = 3
 
@@ -73,12 +73,12 @@ def tile_cvim_pa_t_kernel(tc, x, w1, b1, w2, b2, out):
         def load_x(first, blocks=LOAD_BLOCKS):
             load_rows(x_raw[first // BANK_BLOCKS], first % BANK_BLOCKS, x_rows, first, blocks)
 
-        load_x(0, 1)
-        load_x(1, 1)
-        for first in range(LOAD_BLOCKS, T_BLOCKS, LOAD_BLOCKS):
-            if first == BANK_BLOCKS:
-                load_rows(w_raw, 0, w1, 0)
-            load_x(first)
+        for n in range(BANK_BLOCKS):
+            load_x(n, 1)
+        load_rows(w_raw, 0, w1, 0, 1)
+        for n in range(BANK_BLOCKS, T_BLOCKS, LOAD_BLOCKS):
+            load_x(n)
+        load_rows(w_raw, 1, w1, 1, 1)
         for first in range(0, T_BLOCKS, LOAD_BLOCKS):
             if first + LOAD_BLOCKS < D_TILES:
                 load_rows(w_raw, first + LOAD_BLOCKS, w1, first + LOAD_BLOCKS)
@@ -273,10 +273,12 @@ def tile_cvim_pa_t_kernel(tc, x, w1, b1, w2, b2, out):
         take_x(9)
 
         out_rows = {}
+        returns = {}
+        for s in range(STEPS):
+            returns.setdefault(s + (BACK_LAG if s < STEPS - D_TILES else BACK_LAG - 1), []).append(s)
         for s in range(1, STEPS + BACK_LAG):
             n = T_BLOCKS + X_LEAD + s
             e_next = s + W_AHEAD
-            done = s - BACK_LAG
             multiplies = s < STEPS
             b, e = divmod(s, D_TILES)
 
@@ -294,19 +296,22 @@ def tile_cvim_pa_t_kernel(tc, x, w1, b1, w2, b2, out):
                     for h in range(T_BANKS):
                         outer_tap(e, y_rows[s], acc, j, h)
                 fix_ends(e, y_rows[s])
-            if done >= 0:
+            for done in returns.get(s, []):
                 back = [turn_back(y_rows[done], h) for h in range(T_BANKS)]
                 pair, j = divmod(done, STORE_TILES)
                 if j == 0:
                     out_rows[pair] = wides.tile([P, T_BLOCKS, STORE_TILES * P], F32, name="wide")
                 for h in range(T_BANKS):
                     copy = nc.vector.tensor_copy if (h == 1 and s > STEPS) else nc.scalar.copy
-                    copy(
-                        out=out_rows[pair][:, h * BANK_BLOCKS : (h + 1) * BANK_BLOCKS, j * P : (j + 1) * P],
-                        in_=back[h][:],
-                    )
-                    if done >= STEPS - FINE_STEPS:
-                        store(done // D_TILES, h * BANK, (h + 1) * BANK, done % D_TILES * P, P, out_rows[pair], j * P)
+                    blocks = BANK_BLOCKS // 2 if done == STEPS - 1 else BANK_BLOCKS
+                    for first in range(0, BANK_BLOCKS, blocks):
+                        k = h * BANK_BLOCKS + first
+                        copy(
+                            out=out_rows[pair][:, k : k + blocks, j * P : (j + 1) * P],
+                            in_=back[h][:, first : first + blocks, :],
+                        )
+                        if done >= STEPS - FINE_STEPS:
+                            store(done // D_TILES, k * P, (k + blocks) * P, done % D_TILES * P, P, out_rows[pair], j * P)
                 if j == STORE_TILES - 1 and done < STEPS - FINE_STEPS:
                     store(done // D_TILES, 0, T, (done % D_TILES - j) * P, STORE_TILES * P, out_rows[pair], 0)
             if n < X_BLOCKS:

@@ -33,8 +33,8 @@ X_LEAD = 1
 W_AHEAD = 3
 VECTOR_EVERY = 6
 FINE_STEPS = 8
-WARM_UP = 7
-BACK_LAG = 3
+WARM_UP = 5
+BACK_LAG = 2
 
 FLOPS = 2 * B * T * C * D + 2 * KW * B * T * D
 
@@ -52,8 +52,9 @@ def tile_cvim_pa_t_kernel(tc, x, w1, b1, w2, b2, out):
         accs = pools.enter_context(tc.psum_pool(name="accs", bufs=4))
         turns = pools.enter_context(tc.psum_pool(name="turns", bufs=4))
 
-        zeros = consts.tile([P, BANK], BF16)
-        nc.vector.memset(zeros[:], 0.0)
+        zero_words = consts.tile([P, BANK // 2], F32)
+        nc.vector.memset(zero_words[:], 0.0)
+        zeros = zero_words[:].bitcast(BF16)
         rows = consts.tile([P, KW * P], BF16)
         nc.gpsimd.memset(rows[:], 0.0)
         nc.scalar.dma_start(out=rows[0:B2_ROW, 0:P], in_=b1.rearrange("(e p) -> e p", p=P))
@@ -89,7 +90,7 @@ def tile_cvim_pa_t_kernel(tc, x, w1, b1, w2, b2, out):
         def keep_clock(count):
             for k in range(count):
                 idle = accs.tile([P, BANK], F32, name="acc")
-                nc.tensor.matmul(idle[:], zeros[:, 0:P], zeros[:], start=True, stop=True)
+                nc.tensor.matmul(idle[:], zeros[:, 0:P], zeros, start=True, stop=True)
 
         keep_clock(WARM_UP)
 
@@ -275,7 +276,7 @@ def tile_cvim_pa_t_kernel(tc, x, w1, b1, w2, b2, out):
         out_rows = {}
         returns = {}
         for s in range(STEPS):
-            returns.setdefault(s + (BACK_LAG if s < STEPS - D_TILES else BACK_LAG - 1), []).append(s)
+            returns.setdefault(s + BACK_LAG, []).append(s)
         for s in range(1, STEPS + BACK_LAG):
             n = T_BLOCKS + X_LEAD + s
             e_next = s + W_AHEAD

@@ -31,8 +31,8 @@ STORE_TILES = 2
 STEPS = B * D_TILES
 X_LEAD = 1
 W_AHEAD = 3
-VECTOR_EVERY = 6
-FINE_STEPS = 8
+VECTOR_EVERY = 4
+FINE_STEPS = 12
 WARM_UP = 5
 BACK_LAG = 2
 
@@ -223,7 +223,12 @@ def tile_cvim_pa_t_kernel(tc, x, w1, b1, w2, b2, out):
             return back
 
         def take_x(n, copy=nc.scalar.copy):
-            x_flipped = flip(x_raw[n // BANK_BLOCKS], n % BANK_BLOCKS)
+            lay_x(n, copy, flip_x(n))
+
+        def flip_x(n):
+            return flip(x_raw[n // BANK_BLOCKS], n % BANK_BLOCKS)
+
+        def lay_x(n, copy, x_flipped):
             pair, q = divmod(n, PAIR_BLOCKS)
             if q == 0:
                 x_grouped[pair] = groups.tile(
@@ -288,17 +293,24 @@ def tile_cvim_pa_t_kernel(tc, x, w1, b1, w2, b2, out):
             if e_next - 1 < D_TILES:
                 quantise_w(e_next - 1)
 
+            by_vector = n < X_BLOCKS and n % VECTOR_EVERY == 0
             if multiplies:
                 acc = [multiply(b, e, h) for h in range(T_BANKS)]
                 y_rows[s] = ys.tile([P, T], F32, name="y")
                 for h in range(T_BANKS):
                     middle_tap(e, y_rows[s], acc, h)
-                for j in (0, KW - 1):
-                    for h in range(T_BANKS):
-                        outer_tap(e, y_rows[s], acc, j, h)
+                for h in range(T_BANKS):
+                    outer_tap(e, y_rows[s], acc, 0, h)
+            turned = [(done, [turn_back(y_rows[done], h) for h in range(T_BANKS)]) for done in returns.get(s, [])]
+            if n < X_BLOCKS:
+                x_flipped = flip_x(n)
+            if by_vector:
+                lay_x(n, nc.vector.tensor_copy, x_flipped)
+            if multiplies:
+                for h in range(T_BANKS):
+                    outer_tap(e, y_rows[s], acc, KW - 1, h)
                 fix_ends(e, y_rows[s])
-            for done in returns.get(s, []):
-                back = [turn_back(y_rows[done], h) for h in range(T_BANKS)]
+            for done, back in turned:
                 pair, j = divmod(done, STORE_TILES)
                 if j == 0:
                     out_rows[pair] = wides.tile([P, T_BLOCKS, STORE_TILES * P], F32, name="wide")
@@ -315,7 +327,7 @@ def tile_cvim_pa_t_kernel(tc, x, w1, b1, w2, b2, out):
                             store(done // D_TILES, k * P, (k + blocks) * P, done % D_TILES * P, P, out_rows[pair], j * P)
                 if j == STORE_TILES - 1 and done < STEPS - FINE_STEPS:
                     store(done // D_TILES, 0, T, (done % D_TILES - j) * P, STORE_TILES * P, out_rows[pair], 0)
-            if n < X_BLOCKS:
-                take_x(n, nc.vector.tensor_copy if n % VECTOR_EVERY == 2 else nc.scalar.copy)
+            if n < X_BLOCKS and not by_vector:
+                lay_x(n, nc.scalar.copy, x_flipped)
             if e_next < D_TILES:
                 take_w(e_next)

from contextlib import ExitStack

import concourse.mybir as mybir
from concourse.masks import make_identity

F32 = mybir.dt.float32
BF16 = mybir.dt.bfloat16
U32 = mybir.dt.uint32
U8 = mybir.dt.uint8
FP8X4 = mybir.dt.float8_e4m3fn_x4
ALU = mybir.AluOpType
ACT = mybir.ActivationFunctionType

B, T, C, D, KW = 4, 1024, 1024, 1024, 3
P = 128
PACK = 4
K_PASS = P * PACK
PASSES = C // K_PASS
PAIRS = PACK // 2
BANK = 512
T_BANKS = T // BANK
T_BLOCKS = T // P
X_BLOCKS = B * T_BLOCKS
PAIR_BLOCKS = 2
BANK_BLOCKS = BANK // P
D_TILES = D // P
B2_ROW, W2_ROW = D_TILES, 2 * D_TILES
LOAD_BLOCKS = 2
STORE_TILES = 2

STEPS = B * D_TILES
X_LEAD = 1
W_AHEAD = 3
VECTOR_EVERY = 4
FINE_STEPS = 12
WARM_UP = 5
BACK_LAG = 2

FLOPS = 2 * B * T * C * D + 2 * KW * B * T * D


def tile_cvim_pa_t_kernel(tc, x, w1, b1, w2, b2, out):
    nc = tc.nc
    with ExitStack() as pools:
        pools.enter_context(tc.manual_schedule())
        consts = pools.enter_context(tc.tile_pool(name="consts", bufs=1))
        raws = pools.enter_context(tc.tile_pool(name="raws", bufs=1))
        wides = pools.enter_context(tc.tile_pool(name="wides", bufs=16))
        groups = pools.enter_context(tc.tile_pool(name="groups", bufs=4))
        codes = pools.enter_context(tc.tile_pool(name="codes", bufs=2 * T_BANKS))
        ys = pools.enter_context(tc.tile_pool(name="ys", bufs=BACK_LAG + 2))
        accs = pools.enter_context(tc.psum_pool(name="accs", bufs=4))
        turns = pools.enter_context(tc.psum_pool(name="turns", bufs=4))

        zero_words = consts.tile([P, BANK // 2], F32)
        nc.vector.memset(zero_words[:], 0.0)
        zeros = zero_words[:].bitcast(BF16)
        rows = consts.tile([P, KW * P], BF16)
        nc.gpsimd.memset(rows[:], 0.0)
        nc.scalar.dma_start(out=rows[0:B2_ROW, 0:P], in_=b1.rearrange("(e p) -> e p", p=P))
        nc.scalar.dma_start(out=rows[B2_ROW:W2_ROW, 0:P], in_=b2.rearrange("(e p) -> e p", p=P))
        nc.scalar.dma_start(out=rows[W2_ROW : W2_ROW + D_TILES, :], in_=w2.rearrange("(e p) j -> e (p j)", p=P))

        x_rows = x.flatten_outer_dims()
        x_raw = [wides.tile([P, BANK_BLOCKS * C], BF16, name="wide") for k in range(X_BLOCKS // BANK_BLOCKS)]
        w_raw = raws.tile([P, D_TILES * C], BF16)

        def load_rows(raw, k, rows, first, blocks=LOAD_BLOCKS):
            nc.sync.dma_start(
                out=raw[:].rearrange("p (k c) -> p k c", c=C)[:, k : k + blocks, :],
                in_=rows[first * P : (first + blocks) * P, :].rearrange("(k p) c -> p k c", p=P),
            )

        def load_x(first, blocks=LOAD_BLOCKS):
            load_rows(x_raw[first // BANK_BLOCKS], first % BANK_BLOCKS, x_rows, first, blocks)

        for n in range(BANK_BLOCKS):
            load_x(n, 1)
        load_rows(w_raw, 0, w1, 0, 1)
        for n in range(BANK_BLOCKS, T_BLOCKS, LOAD_BLOCKS):
            load_x(n)
        load_rows(w_raw, 1, w1, 1, 1)
        for first in range(0, T_BLOCKS, LOAD_BLOCKS):
            if first + LOAD_BLOCKS < D_TILES:
                load_rows(w_raw, first + LOAD_BLOCKS, w1, first + LOAD_BLOCKS)
            load_x(T_BLOCKS + first)
        for first in range(2 * T_BLOCKS, X_BLOCKS, LOAD_BLOCKS):
            load_x(first)

        def keep_clock(count):
            for k in range(count):
                idle = accs.tile([P, BANK], F32, name="acc")
                nc.tensor.matmul(idle[:], zeros[:, 0:P], zeros, start=True, stop=True)

        keep_clock(WARM_UP)

        ident = consts.tile([P, P], F32)
        make_identity(nc, ident[:])

        ident_bf16 = consts.tile([P, P], BF16)
        nc.gpsimd.tensor_copy(out=ident_bf16[:], in_=ident[:])

        bias = consts.tile([P, 2, D_TILES], F32)
        taps = consts.tile([P, KW, D_TILES], F32)
        bias_all = consts.tile([P, D_TILES], F32)
        edge = consts.tile([P, D_TILES, 2], F32)

        def prepare_channels():
            columns = turns.tile([P, 1 + KW, P], BF16, tag="turn")
            nc.tensor.transpose(columns[:, 0, :], rows[:, 0:P], ident_bf16[:])
            for j in range(KW):
                nc.tensor.transpose(columns[:, 1 + j, :], rows[:, j : KW * P : KW], ident_bf16[:])
            nc.vector.tensor_copy(
                out=bias[:], in_=columns[:, 0, 0:W2_ROW].rearrange("p (v e) -> p v e", v=2)
            )
            nc.vector.tensor_copy(out=taps[:], in_=columns[:, 1 : 1 + KW, W2_ROW : W2_ROW + D_TILES])
            tap_sum = consts.tile([P, D_TILES], F32)
            nc.gpsimd.tensor_tensor(out=tap_sum[:], in0=taps[:, 0, :], in1=taps[:, 1, :], op=ALU.add)
            nc.gpsimd.tensor_tensor(out=tap_sum[:], in0=tap_sum[:], in1=taps[:, 2, :], op=ALU.add)
            nc.gpsimd.tensor_tensor(out=bias_all[:], in0=tap_sum[:], in1=bias[:, 0, :], op=ALU.mult)
            nc.gpsimd.tensor_tensor(out=bias_all[:], in0=bias_all[:], in1=bias[:, 1, :], op=ALU.add)
            for side in range(2):
                nc.gpsimd.tensor_tensor(
                    out=edge[:, :, side], in0=bias[:, 0, :], in1=taps[:, side * (KW - 1), :], op=ALU.mult
                )
        def flip(raw, block):
            words = raw[:].bitcast(F32)[:, block * (C // 2) : (block + 1) * (C // 2)]
            flipped = turns.tile([P, PASSES, PAIRS, P], F32, tag="turn")
            for g in range(PASSES):
                for u in range(PAIRS):
                    first = g * PAIRS * P + u
                    last = (g + 1) * PAIRS * P
                    nc.tensor.transpose(flipped[:, g, u, :], words[:, first:last:PAIRS], ident[:])
            return flipped

        def regroup(copy, flipped, grouped, n_rows, first_row):
            words = grouped[:].bitcast(F32).rearrange("p (g r u) -> p g r u", g=PASSES, r=n_rows)
            copy(out=words[:, :, first_row : first_row + P, :], in_=flipped[:].rearrange("p g u r -> p g r u"))

        w_codes = consts.tile([P, D_TILES * PASSES * P], U32, align_bytes=64)
        w_scales = consts.tile([P, D_TILES * PASSES * P], U8, align_bytes=64)
        w_grouped = {}

        def quantise_w(e):
            cols = slice(e * PASSES * P, (e + 1) * PASSES * P)
            nc.vector.quantize_mx(
                out=w_codes[:, cols].bitcast(FP8X4), scales=w_scales[:, cols], in_=w_grouped[e][:]
            )

        x_grouped = {}
        x_codes = {}
        x_scales = {}

        def quantise_x(n):
            bank_no, q = divmod(n, BANK_BLOCKS)
            if bank_no not in x_codes:
                x_codes[bank_no] = codes.tile([P, PASSES * BANK], U32, align_bytes=64, name="x_codes")
                x_scales[bank_no] = codes.tile([P, PASSES * BANK], U8, align_bytes=64, name="x_scales")
            width = PAIR_BLOCKS * P
            for g in range(PASSES):
                cols = slice(g * BANK + (q - 1) * P, g * BANK + (q + 1) * P)
                nc.vector.quantize_mx(
                    out=x_codes[bank_no][:, cols].bitcast(FP8X4),
                    scales=x_scales[bank_no][:, cols],
                    in_=x_grouped[n // PAIR_BLOCKS][:, g * width * PACK : (g + 1) * width * PACK],
                )

        def multiply(b, e, h):
            acc = accs.tile([P, BANK], F32, name="acc")
            bank_no = b * T_BANKS + h
            for g in range(PASSES):
                w_cols = slice((e * PASSES + g) * P, (e * PASSES + g + 1) * P)
                x_cols = slice(g * BANK, (g + 1) * BANK)
                nc.tensor.matmul_mx(
                    out=acc[:],
                    lhsT=w_codes[:, w_cols].bitcast(FP8X4),
                    lhsT_scale=w_scales[:, w_cols],
                    rhs=x_codes[bank_no][:, x_cols].bitcast(FP8X4),
                    rhs_scale=x_scales[bank_no][:, x_cols],
                    start=(g == 0),
                    stop=(g == PASSES - 1),
                )
            return acc

        def middle_tap(e, y, acc, h):
            nc.scalar.activation(
                out=y[:, h * BANK : (h + 1) * BANK],
                in_=acc[h][:],
                func=ACT.Identity,
                bias=bias_all[:, e : e + 1],
                scale=taps[:, 1, e : e + 1],
            )

        def outer_tap(e, y, acc, j, h, lo=0, hi=BANK):
            to = h * BANK + 1 - j
            lo = max(lo, -to)
            hi = min(hi, T - to)
            nc.vector.scalar_tensor_tensor(
                out=y[:, to + lo : to + hi],
                in0=acc[h][:, lo:hi],
                scalar=taps[:, j, e : e + 1],
                in1=y[:, to + lo : to + hi],
                op0=ALU.mult,
                op1=ALU.add,
            )

        def fix_ends(e, y):
            nc.gpsimd.tensor_tensor(
                out=y[:, 0 : T : T - 1], in0=y[:, 0 : T : T - 1], in1=edge[:, e, :], op=ALU.subtract
            )

        def store(b, t_lo, t_hi, d_lo, width, rows, col):
            nc.sync.dma_start(
                out=out[b, t_lo:t_hi, d_lo : d_lo + width].rearrange("(k p) d -> p k d", p=P),
                in_=rows[:, t_lo // P : t_hi // P, col : col + width],
            )

        def turn_back(y, h):
            back = turns.tile([P, BANK_BLOCKS, P], F32, tag="turn")
            for i in range(BANK_BLOCKS):
                k = h * BANK_BLOCKS + i
                nc.tensor.transpose(back[:, i, :], y[:, k * P : (k + 1) * P], ident[:])
            return back

        def take_x(n, copy=nc.scalar.copy):
            lay_x(n, copy, flip_x(n))

        def flip_x(n):
            return flip(x_raw[n // BANK_BLOCKS], n % BANK_BLOCKS)

        def lay_x(n, copy, x_flipped):
            pair, q = divmod(n, PAIR_BLOCKS)
            if q == 0:
                x_grouped[pair] = groups.tile(
                    [P, PASSES * PAIR_BLOCKS * P * PACK], BF16, align_bytes=64, name="x_grouped"
                )
            regroup(copy, x_flipped, x_grouped[pair], PAIR_BLOCKS * P, q * P)

        def take_w(e):
            w_flipped = flip(w_raw, e)
            w_grouped[e] = groups.tile([P, PASSES * P * PACK], BF16, align_bytes=64, name="w_grouped")
            regroup(nc.scalar.copy, w_flipped, w_grouped[e], P, 0)

        take_x(0)
        take_x(1)
        keep_clock(1)
        quantise_x(1)
        take_x(2)
        take_x(3)
        prepare_channels()
        keep_clock(1)
        quantise_x(3)
        take_w(0)
        quantise_w(0)
        take_x(4)
        take_x(5)
        quantise_x(5)
        take_x(6)
        y_rows = {0: ys.tile([P, T], F32, name="y")}
        acc = [multiply(0, 0, 0)]
        middle_tap(0, y_rows[0], acc, 0)
        take_x(7)
        take_w(1)
        keep_clock(1)
        outer_tap(0, y_rows[0], acc, 0, 0, hi=BANK - 1)
        quantise_x(7)
        quantise_w(1)
        outer_tap(0, y_rows[0], acc, 2, 0)
        take_w(2)
        take_x(8)
        quantise_w(2)
        acc.append(multiply(0, 0, 1))
        middle_tap(0, y_rows[0], acc, 1)
        outer_tap(0, y_rows[0], acc, 0, 0, lo=BANK - 1)
        outer_tap(0, y_rows[0], acc, 0, 1)
        outer_tap(0, y_rows[0], acc, 2, 1)
        fix_ends(0, y_rows[0])
        take_w(3)
        take_x(9)

        out_rows = {}
        returns = {}
        for s in range(STEPS):
            returns.setdefault(s + BACK_LAG, []).append(s)
        for s in range(1, STEPS + BACK_LAG):
            n = T_BLOCKS + X_LEAD + s
            e_next = s + W_AHEAD
            multiplies = s < STEPS
            b, e = divmod(s, D_TILES)

            if n % 2 == 0 and n - 1 < X_BLOCKS:
                quantise_x(n - 1)
            if e_next - 1 < D_TILES:
                quantise_w(e_next - 1)

            by_vector = n < X_BLOCKS and n % VECTOR_EVERY == 0
            if multiplies:
                acc = [multiply(b, e, h) for h in range(T_BANKS)]
                y_rows[s] = ys.tile([P, T], F32, name="y")
                for h in range(T_BANKS):
                    middle_tap(e, y_rows[s], acc, h)
                for h in range(T_BANKS):
                    outer_tap(e, y_rows[s], acc, 0, h)
            turned = [(done, [turn_back(y_rows[done], h) for h in range(T_BANKS)]) for done in returns.get(s, [])]
            if n < X_BLOCKS:
                x_flipped = flip_x(n)
            if by_vector:
                lay_x(n, nc.vector.tensor_copy, x_flipped)
            if multiplies:
                for h in range(T_BANKS):
                    outer_tap(e, y_rows[s], acc, KW - 1, h)
                fix_ends(e, y_rows[s])
            for done, back in turned:
                pair, j = divmod(done, STORE_TILES)
                if j == 0:
                    out_rows[pair] = wides.tile([P, T_BLOCKS, STORE_TILES * P], F32, name="wide")
                for h in range(T_BANKS):
                    copy = nc.vector.tensor_copy if (h == 1 and s > STEPS) else nc.scalar.copy
                    blocks = BANK_BLOCKS // 2 if done == STEPS - 1 else BANK_BLOCKS
                    for first in range(0, BANK_BLOCKS, blocks):
                        k = h * BANK_BLOCKS + first
                        copy(
                            out=out_rows[pair][:, k : k + blocks, j * P : (j + 1) * P],
                            in_=back[h][:, first : first + blocks, :],
                        )
                        if done >= STEPS - FINE_STEPS:
                            store(done // D_TILES, k * P, (k + blocks) * P, done % D_TILES * P, P, out_rows[pair], j * P)
                if j == STORE_TILES - 1 and done < STEPS - FINE_STEPS:
                    store(done // D_TILES, 0, T, (done % D_TILES - j) * P, STORE_TILES * P, out_rows[pair], 0)
            if n < X_BLOCKS and not by_vector:
                lay_x(n, nc.scalar.copy, x_flipped)
            if e_next < D_TILES:
                take_w(e_next)
